import numpy as np
import ml_dtypes


def mxq(x, axis, fmt="e4m3"):
    dtype, down = {"e4m3": (ml_dtypes.float8_e4m3fn, 7), "e5m2": (ml_dtypes.float8_e5m2, 14)}[fmt]
    v = np.moveaxis(np.asarray(x, np.float32).astype(ml_dtypes.bfloat16).astype(np.float64), axis, -1)
    blocks = v.reshape(v.shape[:-1] + (-1, 32))
    amax = np.abs(blocks).max(-1, keepdims=True)
    byte = np.maximum(np.where(amax > 0, np.frexp(amax)[1] - 1 + 127, 0) - down, 1)
    scale = np.exp2(byte - 127.0)
    codes = (blocks / scale).astype(np.float32).astype(dtype).astype(np.float64)
    return np.moveaxis((codes * scale).reshape(v.shape), -1, axis)


WIDE = False


def mx_kscale(k):
    if not WIDE:
        return np.ones(k)
    levels = np.array([10, -10, 5, -5, 0])
    if k % 512:
        return np.exp2(np.random.permutation(np.resize(levels, k // 32))).repeat(32)
    a = np.empty((k // 512, 16))
    for p in range(k // 512):
        a[p, :8] = np.random.permutation(np.resize(levels, 8))
        for g in range(8):
            far = levels[np.abs(levels - a[p, g]) >= 10]
            a[p, g + 8] = far[np.random.randint(len(far))]
    return np.exp2(a.ravel()).repeat(32)


BF16 = ml_dtypes.bfloat16


def bf(x):
    return np.asarray(x, np.float32).astype(BF16)


def f64(x):
    return np.asarray(x).astype(np.float64)


B, C, N, T, E, O, KCH, ORD = 2, 64, 1024, 12, 10, 64, 3, 2
SIG = 3.0


def setup_inputs():
    s = mx_kscale(N)
    w = np.exp(SIG * np.random.standard_normal((N, N)))
    adj = w / w.sum(-1, keepdims=True)
    return {"x": bf(np.random.standard_normal((B, C, N, T)) / s[None, None, :, None]),
            "adj": bf(adj * s[:, None] / s[None, :])}


def reference(x, adj):
    R = B * C * T
    xr = f64(x).transpose(0, 1, 3, 2).reshape(R, N)
    aq = mxq(f64(adj), 0, "e4m3")
    x1 = mxq(xr, 1, "e4m3") @ aq
    x2 = mxq(x1, 1, "e4m3") @ aq
    return (x1.reshape(B, C, T, N).transpose(0, 1, 3, 2), x2.reshape(B, C, T, N).transpose(0, 1, 3, 2))

@@ -1,0 +1,176 @@
+import concourse.mybir as mybir
+from concourse.masks import make_identity
+
+F32 = mybir.dt.float32
+BF16 = mybir.dt.bfloat16
+U32 = mybir.dt.uint32
+U8 = mybir.dt.uint8
+FP8X4 = mybir.dt.float8_e4m3fn_x4
+
+P = 128
+PACK = 4
+NODES = 1024
+STEPS = 12
+ROWS = 128
+PASSES = NODES // (P * PACK)
+NODE_TILES = NODES // P
+PAIRS = STEPS // 2
+QUARTERS = 4
+STEP_GROUPS = STEPS // QUARTERS
+
+FLOPS = 2 * 2 * ROWS * STEPS * NODES * NODES
+
+
+def copy_out(nc, on_scalar, out, in_):
+    if on_scalar:
+        nc.scalar.copy(out=out, in_=in_)
+    else:
+        nc.vector.tensor_copy(out=out, in_=in_)
+
+
+def hop_to_output(nc, psum, stage, feat_codes, feat_scales, adj_codes, adj_scales, out_rows):
+    for wt in range(NODE_TILES):
+        h, t = divmod(wt, PACK)
+        w_cols = slice(wt * P, (wt + 1) * P)
+        if t == 0:
+            rows = stage.tile([ROWS, P, PACK, STEPS], F32, name="rows")
+        for g in range(STEP_GROUPS):
+            bank = psum.tile([ROWS, QUARTERS, P], F32, name="bank", tag="bank")
+            for i in range(QUARTERS):
+                step = g * QUARTERS + i
+                for c in range(PASSES):
+                    nc.tensor.matmul_mx(
+                        out=bank[:, i, :],
+                        lhsT=feat_codes[:, c, step, :].bitcast(FP8X4),
+                        lhsT_scale=feat_scales[:, c, step, :],
+                        rhs=adj_codes[:, c, w_cols].bitcast(FP8X4),
+                        rhs_scale=adj_scales[:, c, w_cols],
+                        start=(c == 0),
+                        stop=(c == PASSES - 1),
+                    )
+            copy_out(
+                nc,
+                wt % 2 == 0,
+                rows[:, :, t, g * QUARTERS : (g + 1) * QUARTERS],
+                bank[:].rearrange("r i w -> r w i"),
+            )
+        if t == PACK - 1:
+            nc.sync.dma_start(
+                out=out_rows[:, h * PACK * P * STEPS : (h + 1) * PACK * P * STEPS],
+                in_=rows[:].rearrange("r m t l -> r (m t l)"),
+            )
+
+
+def tile_avwgcn_pb_kernel(tc, x, adj, out_0, out_1):
+    nc = tc.nc
+    x_rows = x.rearrange("b c v l -> (b c) (v l)")
+    adj_rows = adj.rearrange("(c p t) w -> p c t w", c=PASSES, t=PACK, p=P)
+    x1_rows = out_0.rearrange("b c w l -> (b c) (w l)")
+    x2_rows = out_1.rearrange("b c w l -> (b c) (w l)")
+    half = NODES * STEPS // PASSES
+
+    with tc.tile_pool(name="keep", bufs=1) as keep, tc.tile_pool(
+        name="mid", bufs=4
+    ) as mid, tc.tile_pool(name="stage", bufs=2) as stage, tc.psum_pool(
+        name="psum", bufs=8
+    ) as psum, tc.manual_schedule():
+        identity = keep.tile([P, P], F32, name="identity")
+        make_identity(nc, identity[:])
+
+        adj_raw = keep.tile([P, PASSES, PACK, NODES], BF16, name="adj_raw")
+        x_raw = keep.tile([ROWS, PASSES, half], BF16, name="x_raw")
+        for c in range(PASSES):
+            nc.sync.dma_start(out=adj_raw[:, c], in_=adj_rows[:, c])
+        for c in range(PASSES):
+            nc.sync.dma_start(out=x_raw[:, c, :], in_=x_rows[:, c * half : (c + 1) * half])
+
+        adj_grouped = keep.tile([P, PASSES, NODES, PACK], BF16, name="adj_grouped", align_bytes=64)
+        adj_codes = keep.tile([P, PASSES, NODES], U32, name="adj_codes", align_bytes=64)
+        adj_scales = keep.tile([P, PASSES, NODES], U8, name="adj_scales", align_bytes=64)
+        for c in range(PASSES):
+            for h in range(PASSES):
+                half_cols = slice(h * PACK * P, (h + 1) * PACK * P)
+                nc.vector.tensor_copy(
+                    out=adj_grouped[:, c, half_cols].rearrange("p (k m) t -> p k m t", k=PACK),
+                    in_=adj_raw[:, c, :, half_cols].rearrange("p t (m k) -> p k m t", k=PACK),
+                )
+        for c in range(PASSES):
+            nc.vector.quantize_mx(
+                out=adj_codes[:, c, :].bitcast(FP8X4),
+                scales=adj_scales[:, c, :],
+                in_=adj_grouped[:, c].rearrange("p w t -> p (w t)"),
+            )
+
+        x_words = x_raw[:].bitcast(F32).rearrange("r c (p t q) -> r c t p q", t=PACK, p=P, q=PAIRS)
+        x_grouped = keep.tile([P, PASSES, STEPS, ROWS, PACK], BF16, name="x_grouped", align_bytes=64)
+        x_codes = keep.tile([P, PASSES, STEPS, ROWS], U32, name="x_codes", align_bytes=64)
+        x_scales = keep.tile([P, PASSES, STEPS, ROWS], U8, name="x_scales", align_bytes=64)
+        for c in range(PASSES):
+            for q in range(PAIRS):
+                bank = psum.tile([P, PACK, ROWS], F32, name="bank", tag="bank")
+                for t in range(PACK):
+                    nc.tensor.transpose(bank[:, t, :], x_words[:, c, t, :, q], identity[:])
+                copy_out(
+                    nc,
+                    q % 3 != 2,
+                    x_grouped[:, c, 2 * q : 2 * q + 2],
+                    bank[:].bitcast(BF16).rearrange("p t (r e) -> p e r t", e=2),
+                )
+                nc.vector.quantize_mx(
+                    out=x_codes[:, c, 2 * q : 2 * q + 2].rearrange("p l r -> p (l r)").bitcast(FP8X4),
+                    scales=x_scales[:, c, 2 * q : 2 * q + 2].rearrange("p l r -> p (l r)"),
+                    in_=x_grouped[:, c, 2 * q : 2 * q + 2].rearrange("p l r t -> p (l r t)"),
+                )
+
+        x1_grouped = keep.tile([P, PASSES, STEPS, ROWS, PACK], BF16, name="x1_grouped", align_bytes=64)
+        x1_codes = keep.tile([P, PASSES, STEPS, ROWS], U32, name="x1_codes", align_bytes=64)
+        x1_scales = keep.tile([P, PASSES, STEPS, ROWS], U8, name="x1_scales", align_bytes=64)
+        for c2 in range(PASSES):
+            sums = []
+            for g in range(STEP_GROUPS):
+                steps = slice(g * QUARTERS, (g + 1) * QUARTERS)
+                x1_t = mid.tile([P, PACK, QUARTERS, ROWS], F32, name="x1_t")
+                sums.append(x1_t)
+                for t in range(PACK):
+                    w_cols = slice((c2 * PACK + t) * P, (c2 * PACK + t + 1) * P)
+                    bank = psum.tile([P, QUARTERS, ROWS], F32, name="bank", tag="bank")
+                    for c in range(PASSES):
+                        nc.tensor.matmul_mx(
+                            out=bank[:].rearrange("p i r -> p (i r)"),
+                            lhsT=adj_codes[:, c, w_cols].bitcast(FP8X4),
+                            lhsT_scale=adj_scales[:, c, w_cols],
+                            rhs=x_codes[:, c, steps].rearrange("p l r -> p (l r)").bitcast(FP8X4),
+                            rhs_scale=x_scales[:, c, steps].rearrange("p l r -> p (l r)"),
+                            start=(c == 0),
+                            stop=(c == PASSES - 1),
+                        )
+                    nc.scalar.copy(out=x1_t[:, t], in_=bank[:])
+                nc.vector.tensor_copy(
+                    out=x1_grouped[:, c2, steps],
+                    in_=x1_t[:].rearrange("p t i r -> p i r t"),
+                )
+                nc.vector.quantize_mx(
+                    out=x1_codes[:, c2, steps].rearrange("p l r -> p (l r)").bitcast(FP8X4),
+                    scales=x1_scales[:, c2, steps].rearrange("p l r -> p (l r)"),
+                    in_=x1_grouped[:, c2, steps].rearrange("p l r t -> p (l r t)"),
+                )
+            for t in range(PACK):
+                wt = c2 * PACK + t
+                if t == 0:
+                    rows = stage.tile([ROWS, P, PACK, STEPS], F32, name="rows")
+                for g in range(STEP_GROUPS):
+                    bank = psum.tile([ROWS, QUARTERS, P], F32, name="bank", tag="bank")
+                    for i in range(QUARTERS):
+                        nc.tensor.transpose(bank[:, i, :], sums[g][:, t, i, :], identity[:])
+                    copy_out(
+                        nc,
+                        wt % 2 == 0,
+                        rows[:, :, t, g * QUARTERS : (g + 1) * QUARTERS],
+                        bank[:].rearrange("r i w -> r w i"),
+                    )
+            nc.sync.dma_start(
+                out=x1_rows[:, c2 * PACK * P * STEPS : (c2 + 1) * PACK * P * STEPS],
+                in_=rows[:].rearrange("r m t l -> r (m t l)"),
+            )
+
+        hop_to_output(nc, psum, stage, x1_codes, x1_scales, adj_codes, adj_scales, x2_rows)

@@ -13,52 +13,14 @@ NODES = 1024
 STEPS = 12
 ROWS = 128
 PASSES = NODES // (P * PACK)
-NODE_TILES = NODES // P
+HALF = P * PACK
 PAIRS = STEPS // 2
 QUARTERS = 4
-STEP_GROUPS = STEPS // QUARTERS
+GROUPS = STEPS // QUARTERS
+TILES = HALF // P
+WORDS = P // PACK
 
 FLOPS = 2 * 2 * ROWS * STEPS * NODES * NODES
-
-
-def copy_out(nc, on_scalar, out, in_):
-    if on_scalar:
-        nc.scalar.copy(out=out, in_=in_)
-    else:
-        nc.vector.tensor_copy(out=out, in_=in_)
-
-
-def hop_to_output(nc, psum, stage, feat_codes, feat_scales, adj_codes, adj_scales, out_rows):
-    for wt in range(NODE_TILES):
-        h, t = divmod(wt, PACK)
-        w_cols = slice(wt * P, (wt + 1) * P)
-        if t == 0:
-            rows = stage.tile([ROWS, P, PACK, STEPS], F32, name="rows")
-        for g in range(STEP_GROUPS):
-            bank = psum.tile([ROWS, QUARTERS, P], F32, name="bank", tag="bank")
-            for i in range(QUARTERS):
-                step = g * QUARTERS + i
-                for c in range(PASSES):
-                    nc.tensor.matmul_mx(
-                        out=bank[:, i, :],
-                        lhsT=feat_codes[:, c, step, :].bitcast(FP8X4),
-                        lhsT_scale=feat_scales[:, c, step, :],
-                        rhs=adj_codes[:, c, w_cols].bitcast(FP8X4),
-                        rhs_scale=adj_scales[:, c, w_cols],
-                        start=(c == 0),
-                        stop=(c == PASSES - 1),
-                    )
-            copy_out(
-                nc,
-                wt % 2 == 0,
-                rows[:, :, t, g * QUARTERS : (g + 1) * QUARTERS],
-                bank[:].rearrange("r i w -> r w i"),
-            )
-        if t == PACK - 1:
-            nc.sync.dma_start(
-                out=out_rows[:, h * PACK * P * STEPS : (h + 1) * PACK * P * STEPS],
-                in_=rows[:].rearrange("r m t l -> r (m t l)"),
-            )
 
 
 def tile_avwgcn_pb_kernel(tc, x, adj, out_0, out_1):
@@ -67,110 +29,224 @@ def tile_avwgcn_pb_kernel(tc, x, adj, out_0, out_1):
     adj_rows = adj.rearrange("(c p t) w -> p c t w", c=PASSES, t=PACK, p=P)
     x1_rows = out_0.rearrange("b c w l -> (b c) (w l)")
     x2_rows = out_1.rearrange("b c w l -> (b c) (w l)")
-    half = NODES * STEPS // PASSES
 
     with tc.tile_pool(name="keep", bufs=1) as keep, tc.tile_pool(
-        name="mid", bufs=4
-    ) as mid, tc.tile_pool(name="stage", bufs=2) as stage, tc.psum_pool(
-        name="psum", bufs=8
-    ) as psum, tc.manual_schedule():
+        name="stage", bufs=9
+    ) as stage, tc.psum_pool(name="psum", bufs=8) as psum, tc.manual_schedule():
         identity = keep.tile([P, P], F32, name="identity")
         make_identity(nc, identity[:])
 
-        adj_raw = keep.tile([P, PASSES, PACK, NODES], BF16, name="adj_raw")
-        x_raw = keep.tile([ROWS, PASSES, half], BF16, name="x_raw")
-        for c in range(PASSES):
-            nc.sync.dma_start(out=adj_raw[:, c], in_=adj_rows[:, c])
-        for c in range(PASSES):
-            nc.sync.dma_start(out=x_raw[:, c, :], in_=x_rows[:, c * half : (c + 1) * half])
-
+        adj_raw = {}
+        for h in range(PASSES):
+            for c in range(PASSES):
+                piece = keep.tile([P, PACK, HALF], BF16, name="piece", tag=f"adj_raw_{c}_{h}")
+                adj_raw[c, h] = piece
         adj_grouped = keep.tile([P, PASSES, NODES, PACK], BF16, name="adj_grouped", align_bytes=64)
         adj_codes = keep.tile([P, PASSES, NODES], U32, name="adj_codes", align_bytes=64)
         adj_scales = keep.tile([P, PASSES, NODES], U8, name="adj_scales", align_bytes=64)
-        for c in range(PASSES):
-            for h in range(PASSES):
-                half_cols = slice(h * PACK * P, (h + 1) * PACK * P)
-                nc.vector.tensor_copy(
-                    out=adj_grouped[:, c, half_cols].rearrange("p (k m) t -> p k m t", k=PACK),
-                    in_=adj_raw[:, c, :, half_cols].rearrange("p t (m k) -> p k m t", k=PACK),
-                )
-        for c in range(PASSES):
-            nc.vector.quantize_mx(
-                out=adj_codes[:, c, :].bitcast(FP8X4),
-                scales=adj_scales[:, c, :],
-                in_=adj_grouped[:, c].rearrange("p w t -> p (w t)"),
-            )
-
-        x_words = x_raw[:].bitcast(F32).rearrange("r c (p t q) -> r c t p q", t=PACK, p=P, q=PAIRS)
+        x_raw = keep.tile([ROWS, PASSES, HALF * STEPS], BF16, name="x_raw")
         x_grouped = keep.tile([P, PASSES, STEPS, ROWS, PACK], BF16, name="x_grouped", align_bytes=64)
         x_codes = keep.tile([P, PASSES, STEPS, ROWS], U32, name="x_codes", align_bytes=64)
         x_scales = keep.tile([P, PASSES, STEPS, ROWS], U8, name="x_scales", align_bytes=64)
-        for c in range(PASSES):
-            for q in range(PAIRS):
-                bank = psum.tile([P, PACK, ROWS], F32, name="bank", tag="bank")
-                for t in range(PACK):
-                    nc.tensor.transpose(bank[:, t, :], x_words[:, c, t, :, q], identity[:])
-                copy_out(
-                    nc,
-                    q % 3 != 2,
-                    x_grouped[:, c, 2 * q : 2 * q + 2],
-                    bank[:].bitcast(BF16).rearrange("p t (r e) -> p e r t", e=2),
-                )
-                nc.vector.quantize_mx(
-                    out=x_codes[:, c, 2 * q : 2 * q + 2].rearrange("p l r -> p (l r)").bitcast(FP8X4),
-                    scales=x_scales[:, c, 2 * q : 2 * q + 2].rearrange("p l r -> p (l r)"),
-                    in_=x_grouped[:, c, 2 * q : 2 * q + 2].rearrange("p l r t -> p (l r t)"),
-                )
-
+        x1_bf16 = keep.tile([ROWS, PASSES, STEPS, 2, P, 2], BF16, name="x1_bf16", align_bytes=64)
         x1_grouped = keep.tile([P, PASSES, STEPS, ROWS, PACK], BF16, name="x1_grouped", align_bytes=64)
         x1_codes = keep.tile([P, PASSES, STEPS, ROWS], U32, name="x1_codes", align_bytes=64)
         x1_scales = keep.tile([P, PASSES, STEPS, ROWS], U8, name="x1_scales", align_bytes=64)
-        for c2 in range(PASSES):
-            sums = []
-            for g in range(STEP_GROUPS):
-                steps = slice(g * QUARTERS, (g + 1) * QUARTERS)
-                x1_t = mid.tile([P, PACK, QUARTERS, ROWS], F32, name="x1_t")
-                sums.append(x1_t)
-                for t in range(PACK):
-                    w_cols = slice((c2 * PACK + t) * P, (c2 * PACK + t + 1) * P)
-                    bank = psum.tile([P, QUARTERS, ROWS], F32, name="bank", tag="bank")
-                    for c in range(PASSES):
-                        nc.tensor.matmul_mx(
-                            out=bank[:].rearrange("p i r -> p (i r)"),
-                            lhsT=adj_codes[:, c, w_cols].bitcast(FP8X4),
-                            lhsT_scale=adj_scales[:, c, w_cols],
-                            rhs=x_codes[:, c, steps].rearrange("p l r -> p (l r)").bitcast(FP8X4),
-                            rhs_scale=x_scales[:, c, steps].rearrange("p l r -> p (l r)"),
-                            start=(c == 0),
-                            stop=(c == PASSES - 1),
-                        )
-                    nc.scalar.copy(out=x1_t[:, t], in_=bank[:])
-                nc.vector.tensor_copy(
-                    out=x1_grouped[:, c2, steps],
-                    in_=x1_t[:].rearrange("p t i r -> p i r t"),
-                )
-                nc.vector.quantize_mx(
-                    out=x1_codes[:, c2, steps].rearrange("p l r -> p (l r)").bitcast(FP8X4),
-                    scales=x1_scales[:, c2, steps].rearrange("p l r -> p (l r)"),
-                    in_=x1_grouped[:, c2, steps].rearrange("p l r t -> p (l r t)"),
-                )
-            for t in range(PACK):
-                wt = c2 * PACK + t
-                if t == 0:
-                    rows = stage.tile([ROWS, P, PACK, STEPS], F32, name="rows")
-                for g in range(STEP_GROUPS):
-                    bank = psum.tile([ROWS, QUARTERS, P], F32, name="bank", tag="bank")
-                    for i in range(QUARTERS):
-                        nc.tensor.transpose(bank[:, i, :], sums[g][:, t, i, :], identity[:])
-                    copy_out(
-                        nc,
-                        wt % 2 == 0,
-                        rows[:, :, t, g * QUARTERS : (g + 1) * QUARTERS],
-                        bank[:].rearrange("r i w -> r w i"),
-                    )
-            nc.sync.dma_start(
-                out=x1_rows[:, c2 * PACK * P * STEPS : (c2 + 1) * PACK * P * STEPS],
-                in_=rows[:].rearrange("r m t l -> r (m t l)"),
+        x_words = x_raw[:].bitcast(F32).rearrange("r c (p t q) -> r c t p q", t=PACK, p=P, q=PAIRS)
+        x1_words = x1_bf16[:].bitcast(F32)
+        x1_grouped_words = x1_grouped[:].bitcast(F32)
+
+        def copy(on_scalar, out, in_):
+            if on_scalar:
+                nc.scalar.copy(out=out, in_=in_)
+            else:
+                nc.vector.tensor_copy(out=out, in_=in_)
+
+        def cols(h):
+            return slice(h * HALF, (h + 1) * HALF)
+
+        def steps(g):
+            return slice(g * QUARTERS, (g + 1) * QUARTERS)
+
+        def adj_load(c, h):
+            nc.sync.dma_start(out=adj_raw[c, h][:], in_=adj_rows[:, c, :, cols(h)])
+
+        def x_load(c):
+            nc.sync.dma_start(out=x_raw[:, c, :], in_=x_rows[:, c * HALF * STEPS : (c + 1) * HALF * STEPS])
+
+        def adj_group(c, h):
+            out = adj_grouped[:, c, cols(h)].rearrange("p (n i) t -> p n t i", i=4)
+            in_ = adj_raw[c, h][:].rearrange("p t (n i) -> p n t i", i=4)
+            if h == 0:
+                nc.vector.tensor_copy(out=out, in_=in_)
+            else:
+                nc.gpsimd.tensor_scalar(out=out, in0=in_, scalar1=1.0, scalar2=0.0, op0=mybir.AluOpType.mult, op1=mybir.AluOpType.add)
+
+        def adj_quant(c, h):
+            nc.vector.quantize_mx(
+                out=adj_codes[:, c, cols(h)].bitcast(FP8X4),
+                scales=adj_scales[:, c, cols(h)],
+                in_=adj_grouped[:, c, cols(h)].rearrange("p w t -> p (w t)"),
             )
 
-        hop_to_output(nc, psum, stage, x1_codes, x1_scales, adj_codes, adj_scales, x2_rows)
+        def quant(grouped, codes, scales, c, g):
+            nc.vector.quantize_mx(
+                out=codes[:, c, steps(g)].rearrange("p l r -> p (l r)").bitcast(FP8X4),
+                scales=scales[:, c, steps(g)].rearrange("p l r -> p (l r)"),
+                in_=grouped[:, c, steps(g)].rearrange("p l r t -> p (l r t)"),
+            )
+
+        def x_quant(c, g):
+            quant(x_grouped, x_codes, x_scales, c, g)
+
+        def x1_quant(c, g):
+            quant(x1_grouped, x1_codes, x1_scales, c, g)
+
+        def x_turn(c, q, on_scalar):
+            bank = psum.tile([P, PACK, ROWS], F32, name="bank", tag="bank")
+            for t in range(PACK):
+                nc.tensor.transpose(bank[:, t, :], x_words[:, c, t, :, q], identity[:])
+            copy(
+                on_scalar,
+                x_grouped[:, c, 2 * q : 2 * q + 2],
+                bank[:].bitcast(BF16).rearrange("p t (r e) -> p e r t", e=2),
+            )
+
+        def hop(codes, scales, g, w0):
+            bank = psum.tile([ROWS, QUARTERS, P], F32, name="bank", tag="bank")
+            for i in range(QUARTERS):
+                for c in range(PASSES):
+                    nc.tensor.matmul_mx(
+                        out=bank[:, i, :],
+                        lhsT=codes[:, c, g * QUARTERS + i, :].bitcast(FP8X4),
+                        lhsT_scale=scales[:, c, g * QUARTERS + i, :],
+                        rhs=adj_codes[:, c, w0 : w0 + P].bitcast(FP8X4),
+                        rhs_scale=adj_scales[:, c, w0 : w0 + P],
+                        start=(c == 0),
+                        stop=(c == PASSES - 1),
+                    )
+            return bank
+
+        def store(out_rows, rows, w0):
+            nc.sync.dma_start(
+                out=out_rows[:, w0 * STEPS : (w0 + P) * STEPS],
+                in_=rows[:].rearrange("r w l -> r (w l)"),
+            )
+
+        rows_of = {}
+
+        def rows_tile(k, wt):
+            if (k, wt) not in rows_of:
+                rows = stage.tile([ROWS, P, STEPS], F32, name="rows")
+                rows_of[(k, wt)] = rows
+            return rows_of[(k, wt)]
+
+        def hop1(h, g, j, rows_on_scalar):
+            wt = h * TILES + j
+            bank = hop(x_codes, x_scales, g, wt * P)
+            rows = rows_tile(0, wt)
+            copy(rows_on_scalar, rows[:, :, steps(g)], bank[:].rearrange("r l w -> r w l"))
+            words = slice(j * WORDS, (j + 1) * WORDS)
+            if h == 1:
+                copy(
+                    not rows_on_scalar,
+                    x1_bf16[:, h, steps(g), :, words, :].rearrange("r l u p e -> r u l p e"),
+                    bank[:].rearrange("r l (p u e) -> r u l p e", u=2, e=2),
+                )
+            if g == GROUPS - 1:
+                store(x1_rows, rows, wt * P)
+                if h == 0:
+                    nodes = rows[:].rearrange("r (p u e) l -> r u l p e", u=2, e=2)
+                    for u in range(2):
+                        nc.gpsimd.tensor_scalar(
+                            out=x1_bf16[:, h, :, u, words, :],
+                            in0=nodes[:, u],
+                            scalar1=1.0,
+                            scalar2=0.0,
+                            op0=mybir.AluOpType.mult,
+                            op1=mybir.AluOpType.add,
+                        )
+
+        def x1_turn(h, g, sides):
+            for l, on_scalar in zip((g * QUARTERS, g * QUARTERS + 2), sides):
+                bank = psum.tile([P, 2, 2, ROWS], F32, name="bank", tag="bank")
+                for i in range(2):
+                    for u in range(2):
+                        nc.tensor.transpose(bank[:, i, u, :], x1_words[:, h, l + i, u, :, 0], identity[:])
+                copy(on_scalar, x1_grouped_words[:, h, l : l + 2], bank[:].rearrange("p l u r -> p l r u"))
+
+        def hop2(wt, g, on_scalar):
+            bank = hop(x1_codes, x1_scales, g, wt * P)
+            rows = rows_tile(1, wt)
+            copy(on_scalar, rows[:, :, steps(g)], bank[:].rearrange("r l w -> r w l"))
+            if g == GROUPS - 1:
+                store(x2_rows, rows, wt * P)
+
+        adj_load(0, 0)
+        x_load(0)
+        adj_load(1, 0)
+        x_load(1)
+        adj_load(0, 1)
+        adj_load(1, 1)
+        adj_group(0, 1)
+        adj_group(1, 1)
+
+        adj_group(0, 0)
+        adj_quant(0, 0)
+        x_turn(0, 0, True)
+        x_turn(0, 1, False)
+        x_turn(0, 2, True)
+        x_turn(0, 3, False)
+        x_quant(0, 0)
+        x_turn(0, 4, True)
+        x_turn(0, 5, True)
+        adj_group(1, 0)
+        x_turn(1, 0, True)
+        x_turn(1, 1, False)
+        adj_quant(1, 0)
+        x_quant(1, 0)
+        x_turn(1, 2, True)
+        x_turn(1, 3, False)
+        x_quant(0, 1)
+        x_turn(1, 4, True)
+        x_quant(1, 1)
+        x_turn(1, 5, True)
+        x_quant(0, 2)
+
+        for j in range(TILES):
+            hop1(0, 0, j, j % 2 == 0)
+            if j == 0:
+                x_quant(1, 2)
+        adj_quant(0, 1)
+        for j in (0, 1):
+            hop1(0, 1, j, j % 2 == 0)
+        for j in (0, 1):
+            hop1(0, 2, j, j % 2 == 0)
+        adj_quant(1, 1)
+        for j in (2, 3):
+            for g in (1, 2):
+                hop1(0, g, j, j % 2 == 0)
+
+        for g in range(GROUPS):
+            for j in range(TILES):
+                hop1(1, g, j, True)
+
+        x1_turn(0, 0, (True, True))
+        x1_turn(1, 0, (True, False))
+        x1_quant(0, 0)
+        x1_turn(0, 1, (True, False))
+        x1_quant(1, 0)
+        x1_turn(1, 1, (True, True))
+        x1_quant(0, 1)
+        x1_turn(0, 2, (True, False))
+        x1_quant(1, 1)
+        x1_turn(1, 2, (True, True))
+        x1_quant(0, 2)
+        x1_quant(1, 2)
+
+        for g in range(GROUPS):
+            for wt in range(2):
+                hop2(wt, g, wt % 2 == 0)
+        for wt in range(2, 2 * TILES):
+            for g in range(GROUPS):
+                hop2(wt, g, wt % 2 == 0)

@@ -77,10 +77,7 @@ def tile_avwgcn_pb_kernel(tc, x, adj, out_0, out_1):
         def adj_group(c, h):
             out = adj_grouped[:, c, cols(h)].rearrange("p (n i) t -> p n t i", i=4)
             in_ = adj_raw[c, h][:].rearrange("p t (n i) -> p n t i", i=4)
-            if h == 0:
-                nc.vector.tensor_copy(out=out, in_=in_)
-            else:
-                nc.gpsimd.tensor_scalar(out=out, in0=in_, scalar1=1.0, scalar2=0.0, op0=mybir.AluOpType.mult, op1=mybir.AluOpType.add)
+            nc.vector.tensor_copy(out=out, in_=in_)
 
         def adj_quant(c, h):
             nc.vector.quantize_mx(
@@ -141,31 +138,19 @@ def tile_avwgcn_pb_kernel(tc, x, adj, out_0, out_1):
                 rows_of[(k, wt)] = rows
             return rows_of[(k, wt)]
 
-        def hop1(h, g, j, rows_on_scalar):
+        def hop1(h, g, j, rows_on_scalar, cast_on_scalar):
             wt = h * TILES + j
             bank = hop(x_codes, x_scales, g, wt * P)
             rows = rows_tile(0, wt)
             copy(rows_on_scalar, rows[:, :, steps(g)], bank[:].rearrange("r l w -> r w l"))
             words = slice(j * WORDS, (j + 1) * WORDS)
-            if h == 1:
-                copy(
-                    not rows_on_scalar,
-                    x1_bf16[:, h, steps(g), :, words, :].rearrange("r l u p e -> r u l p e"),
-                    bank[:].rearrange("r l (p u e) -> r u l p e", u=2, e=2),
-                )
+            copy(
+                cast_on_scalar,
+                x1_bf16[:, h, steps(g), :, words, :].rearrange("r l u p e -> r u l p e"),
+                bank[:].rearrange("r l (p u e) -> r u l p e", u=2, e=2),
+            )
             if g == GROUPS - 1:
                 store(x1_rows, rows, wt * P)
-                if h == 0:
-                    nodes = rows[:].rearrange("r (p u e) l -> r u l p e", u=2, e=2)
-                    for u in range(2):
-                        nc.gpsimd.tensor_scalar(
-                            out=x1_bf16[:, h, :, u, words, :],
-                            in0=nodes[:, u],
-                            scalar1=1.0,
-                            scalar2=0.0,
-                            op0=mybir.AluOpType.mult,
-                            op1=mybir.AluOpType.add,
-                        )
 
         def x1_turn(h, g, sides):
             for l, on_scalar in zip((g * QUARTERS, g * QUARTERS + 2), sides):
@@ -188,8 +173,6 @@ def tile_avwgcn_pb_kernel(tc, x, adj, out_0, out_1):
         x_load(1)
         adj_load(0, 1)
         adj_load(1, 1)
-        adj_group(0, 1)
-        adj_group(1, 1)
 
         adj_group(0, 0)
         adj_quant(0, 0)
@@ -214,22 +197,21 @@ def tile_avwgcn_pb_kernel(tc, x, adj, out_0, out_1):
         x_quant(0, 2)
 
         for j in range(TILES):
-            hop1(0, 0, j, j % 2 == 0)
+            hop1(0, 0, j, True, False)
             if j == 0:
                 x_quant(1, 2)
+        adj_group(0, 1)
         adj_quant(0, 1)
-        for j in (0, 1):
-            hop1(0, 1, j, j % 2 == 0)
-        for j in (0, 1):
-            hop1(0, 2, j, j % 2 == 0)
+        adj_group(1, 1)
         adj_quant(1, 1)
-        for j in (2, 3):
-            for g in (1, 2):
-                hop1(0, g, j, j % 2 == 0)
+        for j in range(TILES):
+            hop1(0, 1, j, True, True)
+        for j in range(TILES):
+            hop1(0, 2, j, True, False)
 
         for g in range(GROUPS):
             for j in range(TILES):
-                hop1(1, g, j, True)
+                hop1(1, g, j, True, False)
 
         x1_turn(0, 0, (True, True))
         x1_turn(1, 0, (True, False))

@@ -31,7 +31,7 @@ def tile_avwgcn_pb_kernel(tc, x, adj, out_0, out_1):
     x2_rows = out_1.rearrange("b c w l -> (b c) (w l)")
 
     with tc.tile_pool(name="keep", bufs=1) as keep, tc.tile_pool(
-        name="stage", bufs=9
+        name="stage", bufs=6
     ) as stage, tc.psum_pool(name="psum", bufs=8) as psum, tc.manual_schedule():
         identity = keep.tile([P, P], F32, name="identity")
         make_identity(nc, identity[:])
@@ -45,16 +45,18 @@ def tile_avwgcn_pb_kernel(tc, x, adj, out_0, out_1):
         adj_codes = keep.tile([P, PASSES, NODES], U32, name="adj_codes", align_bytes=64)
         adj_scales = keep.tile([P, PASSES, NODES], U8, name="adj_scales", align_bytes=64)
         x_raw = keep.tile([ROWS, PASSES, HALF * STEPS], BF16, name="x_raw")
-        x_grouped = keep.tile([P, PASSES, STEPS, ROWS, PACK], BF16, name="x_grouped", align_bytes=64)
+        x_grouped = keep.tile([P, PASSES, STEPS, ROWS, PACK], BF16, name="x_grouped", tag="grouped", align_bytes=64)
         x_codes = keep.tile([P, PASSES, STEPS, ROWS], U32, name="x_codes", align_bytes=64)
         x_scales = keep.tile([P, PASSES, STEPS, ROWS], U8, name="x_scales", align_bytes=64)
         x1_bf16 = keep.tile([ROWS, PASSES, STEPS, 2, P, 2], BF16, name="x1_bf16", align_bytes=64)
-        x1_grouped = keep.tile([P, PASSES, STEPS, ROWS, PACK], BF16, name="x1_grouped", align_bytes=64)
         x1_codes = keep.tile([P, PASSES, STEPS, ROWS], U32, name="x1_codes", align_bytes=64)
         x1_scales = keep.tile([P, PASSES, STEPS, ROWS], U8, name="x1_scales", align_bytes=64)
+        x1_first = []
+        for h in range(PASSES):
+            nodes = keep.tile([ROWS, HALF, STEPS], F32, name="nodes", tag=f"x1_first_{h}")
+            x1_first.append(nodes)
         x_words = x_raw[:].bitcast(F32).rearrange("r c (p t q) -> r c t p q", t=PACK, p=P, q=PAIRS)
         x1_words = x1_bf16[:].bitcast(F32)
-        x1_grouped_words = x1_grouped[:].bitcast(F32)
 
         def copy(on_scalar, out, in_):
             if on_scalar:
@@ -127,7 +129,7 @@ def tile_avwgcn_pb_kernel(tc, x, adj, out_0, out_1):
         def store(out_rows, rows, w0):
             nc.sync.dma_start(
                 out=out_rows[:, w0 * STEPS : (w0 + P) * STEPS],
-                in_=rows[:].rearrange("r w l -> r (w l)"),
+                in_=rows.rearrange("r w l -> r (w l)"),
             )
 
         rows_of = {}
@@ -138,19 +140,20 @@ def tile_avwgcn_pb_kernel(tc, x, adj, out_0, out_1):
                 rows_of[(k, wt)] = rows
             return rows_of[(k, wt)]
 
-        def hop1(h, g, j, rows_on_scalar, cast_on_scalar):
-            wt = h * TILES + j
-            bank = hop(x_codes, x_scales, g, wt * P)
-            rows = rows_tile(0, wt)
-            copy(rows_on_scalar, rows[:, :, steps(g)], bank[:].rearrange("r l w -> r w l"))
-            words = slice(j * WORDS, (j + 1) * WORDS)
-            copy(
-                cast_on_scalar,
-                x1_bf16[:, h, steps(g), :, words, :].rearrange("r l u p e -> r u l p e"),
-                bank[:].rearrange("r l (p u e) -> r u l p e", u=2, e=2),
-            )
+        def hop1(h, g, j, on_scalar):
+            bank = hop(x_codes, x_scales, g, (h * TILES + j) * P)
+            nodes = x1_first[h][:, j * P : (j + 1) * P, :]
+            copy(on_scalar, nodes[:, :, steps(g)], bank[:].rearrange("r l w -> r w l"))
             if g == GROUPS - 1:
-                store(x1_rows, rows, wt * P)
+                store(x1_rows, nodes, (h * TILES + j) * P)
+
+        def x1_round(h, g):
+            nodes = x1_first[h][:].rearrange("r (p u e) l -> r u p e l", u=2, e=2)
+            for u in range(2):
+                nc.vector.tensor_copy(
+                    out=x1_bf16[:, h, steps(g), u].rearrange("r l p e -> r p e l"),
+                    in_=nodes[:, u, :, :, steps(g)],
+                )
 
         def x1_turn(h, g, sides):
             for l, on_scalar in zip((g * QUARTERS, g * QUARTERS + 2), sides):
@@ -158,14 +161,14 @@ def tile_avwgcn_pb_kernel(tc, x, adj, out_0, out_1):
                 for i in range(2):
                     for u in range(2):
                         nc.tensor.transpose(bank[:, i, u, :], x1_words[:, h, l + i, u, :, 0], identity[:])
-                copy(on_scalar, x1_grouped_words[:, h, l : l + 2], bank[:].rearrange("p l u r -> p l r u"))
+                copy(on_scalar, x1_grouped[:].bitcast(F32)[:, h, l : l + 2], bank[:].rearrange("p l u r -> p l r u"))
 
         def hop2(wt, g, on_scalar):
             bank = hop(x1_codes, x1_scales, g, wt * P)
             rows = rows_tile(1, wt)
             copy(on_scalar, rows[:, :, steps(g)], bank[:].rearrange("r l w -> r w l"))
             if g == GROUPS - 1:
-                store(x2_rows, rows, wt * P)
+                store(x2_rows, rows[:], wt * P)
 
         adj_load(0, 0)
         x_load(0)
@@ -196,8 +199,10 @@ def tile_avwgcn_pb_kernel(tc, x, adj, out_0, out_1):
         x_turn(1, 5, True)
         x_quant(0, 2)
 
+        x1_grouped = keep.tile([P, PASSES, STEPS, ROWS, PACK], BF16, name="x1_grouped", tag="grouped", align_bytes=64)
+
         for j in range(TILES):
-            hop1(0, 0, j, True, False)
+            hop1(0, 0, j, True)
             if j == 0:
                 x_quant(1, 2)
         adj_group(0, 1)
@@ -205,18 +210,27 @@ def tile_avwgcn_pb_kernel(tc, x, adj, out_0, out_1):
         adj_group(1, 1)
         adj_quant(1, 1)
         for j in range(TILES):
-            hop1(0, 1, j, True, True)
+            hop1(0, 1, j, True)
+        x1_round(0, 0)
         for j in range(TILES):
-            hop1(0, 2, j, True, False)
+            hop1(0, 2, j, True)
+        x1_round(0, 1)
 
-        for g in range(GROUPS):
-            for j in range(TILES):
-                hop1(1, g, j, True, False)
+        for j in range(TILES):
+            hop1(1, 0, j, j % 2 == 0)
+        x1_round(0, 2)
+        for j in range(TILES):
+            hop1(1, 1, j, j % 2 == 0)
+        x1_round(1, 0)
+        for j in range(TILES):
+            hop1(1, 2, j, j % 2 == 0)
+        x1_round(1, 1)
+        x1_round(1, 2)
 
         x1_turn(0, 0, (True, True))
-        x1_turn(1, 0, (True, False))
+        x1_turn(1, 0, (True, True))
         x1_quant(0, 0)
-        x1_turn(0, 1, (True, False))
+        x1_turn(0, 1, (True, True))
         x1_quant(1, 0)
         x1_turn(1, 1, (True, True))
         x1_quant(0, 1)

@@ -198,13 +198,12 @@ def tile_avwgcn_pb_kernel(tc, x, adj, out_0, out_1):
         x_quant(1, 1)
         x_turn(1, 5, True)
         x_quant(0, 2)
+        x_quant(1, 2)
 
         x1_grouped = keep.tile([P, PASSES, STEPS, ROWS, PACK], BF16, name="x1_grouped", tag="grouped", align_bytes=64)
 
         for j in range(TILES):
             hop1(0, 0, j, True)
-            if j == 0:
-                x_quant(1, 2)
         adj_group(0, 1)
         adj_quant(0, 1)
         adj_group(1, 1)
@@ -215,22 +214,20 @@ def tile_avwgcn_pb_kernel(tc, x, adj, out_0, out_1):
         for j in range(TILES):
             hop1(0, 2, j, True)
         x1_round(0, 1)
-
         for j in range(TILES):
-            hop1(1, 0, j, j % 2 == 0)
+            hop1(1, 0, j, True)
         x1_round(0, 2)
         for j in range(TILES):
-            hop1(1, 1, j, j % 2 == 0)
+            hop1(1, 1, j, True)
         x1_round(1, 0)
         for j in range(TILES):
-            hop1(1, 2, j, j % 2 == 0)
+            hop1(1, 2, j, True)
         x1_round(1, 1)
         x1_round(1, 2)
-
         x1_turn(0, 0, (True, True))
         x1_turn(1, 0, (True, True))
         x1_quant(0, 0)
-        x1_turn(0, 1, (True, True))
+        x1_turn(0, 1, (True, False))
         x1_quant(1, 0)
         x1_turn(1, 1, (True, True))
         x1_quant(0, 1)
@@ -239,10 +236,12 @@ def tile_avwgcn_pb_kernel(tc, x, adj, out_0, out_1):
         x1_turn(1, 2, (True, True))
         x1_quant(0, 2)
         x1_quant(1, 2)
-
-        for g in range(GROUPS):
-            for wt in range(2):
-                hop2(wt, g, wt % 2 == 0)
+        hop2(0, 0, True)
+        hop2(1, 0, False)
+        hop2(0, 1, True)
+        hop2(1, 1, False)
+        hop2(0, 2, True)
+        hop2(1, 2, False)
         for wt in range(2, 2 * TILES):
             for g in range(GROUPS):
                 hop2(wt, g, wt % 2 == 0)

import concourse.mybir as mybir
from concourse.masks import make_identity

F32 = mybir.dt.float32
BF16 = mybir.dt.bfloat16
U32 = mybir.dt.uint32
U8 = mybir.dt.uint8
FP8X4 = mybir.dt.float8_e4m3fn_x4

P = 128
PACK = 4
NODES = 1024
STEPS = 12
ROWS = 128
PASSES = NODES // (P * PACK)
HALF = P * PACK
PAIRS = STEPS // 2
QUARTERS = 4
GROUPS = STEPS // QUARTERS
TILES = HALF // P
WORDS = P // PACK

FLOPS = 2 * 2 * ROWS * STEPS * NODES * NODES


def tile_avwgcn_pb_kernel(tc, x, adj, out_0, out_1):
    nc = tc.nc
    x_rows = x.rearrange("b c v l -> (b c) (v l)")
    adj_rows = adj.rearrange("(c p t) w -> p c t w", c=PASSES, t=PACK, p=P)
    x1_rows = out_0.rearrange("b c w l -> (b c) (w l)")
    x2_rows = out_1.rearrange("b c w l -> (b c) (w l)")

    with tc.tile_pool(name="keep", bufs=1) as keep, tc.tile_pool(
        name="stage", bufs=6
    ) as stage, tc.psum_pool(name="psum", bufs=8) as psum, tc.manual_schedule():
        identity = keep.tile([P, P], F32, name="identity")
        make_identity(nc, identity[:])

        adj_raw = {}
        for h in range(PASSES):
            for c in range(PASSES):
                piece = keep.tile([P, PACK, HALF], BF16, name="piece", tag=f"adj_raw_{c}_{h}")
                adj_raw[c, h] = piece
        adj_grouped = keep.tile([P, PASSES, NODES, PACK], BF16, name="adj_grouped", align_bytes=64)
        adj_codes = keep.tile([P, PASSES, NODES], U32, name="adj_codes", align_bytes=64)
        adj_scales = keep.tile([P, PASSES, NODES], U8, name="adj_scales", align_bytes=64)
        x_raw = keep.tile([ROWS, PASSES, HALF * STEPS], BF16, name="x_raw")
        x_grouped = keep.tile([P, PASSES, STEPS, ROWS, PACK], BF16, name="x_grouped", tag="grouped", align_bytes=64)
        x_codes = keep.tile([P, PASSES, STEPS, ROWS], U32, name="x_codes", align_bytes=64)
        x_scales = keep.tile([P, PASSES, STEPS, ROWS], U8, name="x_scales", align_bytes=64)
        x1_bf16 = keep.tile([ROWS, PASSES, STEPS, 2, P, 2], BF16, name="x1_bf16", align_bytes=64)
        x1_codes = keep.tile([P, PASSES, STEPS, ROWS], U32, name="x1_codes", align_bytes=64)
        x1_scales = keep.tile([P, PASSES, STEPS, ROWS], U8, name="x1_scales", align_bytes=64)
        x1_first = []
        for h in range(PASSES):
            nodes = keep.tile([ROWS, HALF, STEPS], F32, name="nodes", tag=f"x1_first_{h}")
            x1_first.append(nodes)
        x_words = x_raw[:].bitcast(F32).rearrange("r c (p t q) -> r c t p q", t=PACK, p=P, q=PAIRS)
        x1_words = x1_bf16[:].bitcast(F32)

        def copy(on_scalar, out, in_):
            if on_scalar:
                nc.scalar.copy(out=out, in_=in_)
            else:
                nc.vector.tensor_copy(out=out, in_=in_)

        def cols(h):
            return slice(h * HALF, (h + 1) * HALF)

        def steps(g):
            return slice(g * QUARTERS, (g + 1) * QUARTERS)

        def adj_load(c, h):
            nc.sync.dma_start(out=adj_raw[c, h][:], in_=adj_rows[:, c, :, cols(h)])

        def x_load(c):
            nc.sync.dma_start(out=x_raw[:, c, :], in_=x_rows[:, c * HALF * STEPS : (c + 1) * HALF * STEPS])

        def adj_group(c, h):
            out = adj_grouped[:, c, cols(h)].rearrange("p (n i) t -> p n t i", i=4)
            in_ = adj_raw[c, h][:].rearrange("p t (n i) -> p n t i", i=4)
            nc.vector.tensor_copy(out=out, in_=in_)

        def adj_quant(c, h):
            nc.vector.quantize_mx(
                out=adj_codes[:, c, cols(h)].bitcast(FP8X4),
                scales=adj_scales[:, c, cols(h)],
                in_=adj_grouped[:, c, cols(h)].rearrange("p w t -> p (w t)"),
            )

        def quant(grouped, codes, scales, c, g):
            nc.vector.quantize_mx(
                out=codes[:, c, steps(g)].rearrange("p l r -> p (l r)").bitcast(FP8X4),
                scales=scales[:, c, steps(g)].rearrange("p l r -> p (l r)"),
                in_=grouped[:, c, steps(g)].rearrange("p l r t -> p (l r t)"),
            )

        def x_quant(c, g):
            quant(x_grouped, x_codes, x_scales, c, g)

        def x1_quant(c, g):
            quant(x1_grouped, x1_codes, x1_scales, c, g)

        def x_turn(c, q, on_scalar):
            bank = psum.tile([P, PACK, ROWS], F32, name="bank", tag="bank")
            for t in range(PACK):
                nc.tensor.transpose(bank[:, t, :], x_words[:, c, t, :, q], identity[:])
            copy(
                on_scalar,
                x_grouped[:, c, 2 * q : 2 * q + 2],
                bank[:].bitcast(BF16).rearrange("p t (r e) -> p e r t", e=2),
            )

        def hop(codes, scales, g, w0):
            bank = psum.tile([ROWS, QUARTERS, P], F32, name="bank", tag="bank")
            for i in range(QUARTERS):
                for c in range(PASSES):
                    nc.tensor.matmul_mx(
                        out=bank[:, i, :],
                        lhsT=codes[:, c, g * QUARTERS + i, :].bitcast(FP8X4),
                        lhsT_scale=scales[:, c, g * QUARTERS + i, :],
                        rhs=adj_codes[:, c, w0 : w0 + P].bitcast(FP8X4),
                        rhs_scale=adj_scales[:, c, w0 : w0 + P],
                        start=(c == 0),
                        stop=(c == PASSES - 1),
                    )
            return bank

        def store(out_rows, rows, w0):
            nc.sync.dma_start(
                out=out_rows[:, w0 * STEPS : (w0 + P) * STEPS],
                in_=rows.rearrange("r w l -> r (w l)"),
            )

        rows_of = {}

        def rows_tile(k, wt):
            if (k, wt) not in rows_of:
                rows = stage.tile([ROWS, P, STEPS], F32, name="rows")
                rows_of[(k, wt)] = rows
            return rows_of[(k, wt)]

        def hop1(h, g, j, on_scalar):
            bank = hop(x_codes, x_scales, g, (h * TILES + j) * P)
            nodes = x1_first[h][:, j * P : (j + 1) * P, :]
            copy(on_scalar, nodes[:, :, steps(g)], bank[:].rearrange("r l w -> r w l"))
            if g == GROUPS - 1:
                store(x1_rows, nodes, (h * TILES + j) * P)

        def x1_round(h, g):
            nodes = x1_first[h][:].rearrange("r (p u e) l -> r u p e l", u=2, e=2)
            for u in range(2):
                nc.vector.tensor_copy(
                    out=x1_bf16[:, h, steps(g), u].rearrange("r l p e -> r p e l"),
                    in_=nodes[:, u, :, :, steps(g)],
                )

        def x1_turn(h, g, sides):
            for l, on_scalar in zip((g * QUARTERS, g * QUARTERS + 2), sides):
                bank = psum.tile([P, 2, 2, ROWS], F32, name="bank", tag="bank")
                for i in range(2):
                    for u in range(2):
                        nc.tensor.transpose(bank[:, i, u, :], x1_words[:, h, l + i, u, :, 0], identity[:])
                copy(on_scalar, x1_grouped[:].bitcast(F32)[:, h, l : l + 2], bank[:].rearrange("p l u r -> p l r u"))

        def hop2(wt, g, on_scalar):
            bank = hop(x1_codes, x1_scales, g, wt * P)
            rows = rows_tile(1, wt)
            copy(on_scalar, rows[:, :, steps(g)], bank[:].rearrange("r l w -> r w l"))
            if g == GROUPS - 1:
                store(x2_rows, rows[:], wt * P)

        adj_load(0, 0)
        x_load(0)
        adj_load(1, 0)
        x_load(1)
        adj_load(0, 1)
        adj_load(1, 1)

        adj_group(0, 0)
        adj_quant(0, 0)
        x_turn(0, 0, True)
        x_turn(0, 1, False)
        x_turn(0, 2, True)
        x_turn(0, 3, False)
        x_quant(0, 0)
        x_turn(0, 4, True)
        x_turn(0, 5, True)
        adj_group(1, 0)
        x_turn(1, 0, True)
        x_turn(1, 1, False)
        adj_quant(1, 0)
        x_quant(1, 0)
        x_turn(1, 2, True)
        x_turn(1, 3, False)
        x_quant(0, 1)
        x_turn(1, 4, True)
        x_quant(1, 1)
        x_turn(1, 5, True)
        x_quant(0, 2)
        x_quant(1, 2)

        x1_grouped = keep.tile([P, PASSES, STEPS, ROWS, PACK], BF16, name="x1_grouped", tag="grouped", align_bytes=64)

        for j in range(TILES):
            hop1(0, 0, j, True)
        adj_group(0, 1)
        adj_quant(0, 1)
        adj_group(1, 1)
        adj_quant(1, 1)
        for j in range(TILES):
            hop1(0, 1, j, True)
        x1_round(0, 0)
        for j in range(TILES):
            hop1(0, 2, j, True)
        x1_round(0, 1)
        for j in range(TILES):
            hop1(1, 0, j, True)
        x1_round(0, 2)
        for j in range(TILES):
            hop1(1, 1, j, True)
        x1_round(1, 0)
        for j in range(TILES):
            hop1(1, 2, j, True)
        x1_round(1, 1)
        x1_round(1, 2)
        x1_turn(0, 0, (True, True))
        x1_turn(1, 0, (True, True))
        x1_quant(0, 0)
        x1_turn(0, 1, (True, False))
        x1_quant(1, 0)
        x1_turn(1, 1, (True, True))
        x1_quant(0, 1)
        x1_turn(0, 2, (True, False))
        x1_quant(1, 1)
        x1_turn(1, 2, (True, True))
        x1_quant(0, 2)
        x1_quant(1, 2)
        hop2(0, 0, True)
        hop2(1, 0, False)
        hop2(0, 1, True)
        hop2(1, 1, False)
        hop2(0, 2, True)
        hop2(1, 2, False)
        for wt in range(2, 2 * TILES):
            for g in range(GROUPS):
                hop2(wt, g, wt % 2 == 0)
